import numpy as np
import ml_dtypes


def mxq(x, axis, fmt="e4m3"):
    dtype, down = {"e4m3": (ml_dtypes.float8_e4m3fn, 7), "e5m2": (ml_dtypes.float8_e5m2, 14)}[fmt]
    v = np.moveaxis(np.asarray(x, np.float32).astype(ml_dtypes.bfloat16).astype(np.float64), axis, -1)
    blocks = v.reshape(v.shape[:-1] + (-1, 32))
    amax = np.abs(blocks).max(-1, keepdims=True)
    byte = np.maximum(np.where(amax > 0, np.frexp(amax)[1] - 1 + 127, 0) - down, 1)
    scale = np.exp2(byte - 127.0)
    codes = (blocks / scale).astype(np.float32).astype(dtype).astype(np.float64)
    return np.moveaxis((codes * scale).reshape(v.shape), -1, axis)


WIDE = False


def mx_kscale(k):
    if not WIDE:
        return np.ones(k)
    levels = np.array([10, -10, 5, -5, 0])
    a = np.random.permutation(np.resize(levels, k // 512 * 4)).reshape(k // 512, 4)
    idx = np.arange(k)
    return np.exp2(a[idx // 512, idx % 128 // 32])


BF16 = ml_dtypes.bfloat16


def bf(x):
    return np.asarray(x, np.float32).astype(BF16)


def f64(x):
    return np.asarray(x).astype(np.float64)


E, N, D, H = 4, 2048, 128, 512
NEG_SLOPE = 0.01


def leaky_relu(v):
    return np.where(v >= 0, v, NEG_SLOPE * v)


def setup_inputs():
    t, u = mx_kscale(H), mx_kscale(H)
    return {"x": bf(np.random.standard_normal((E, N, D))),
            "w1": bf(np.random.standard_normal((E, D, H)) / np.sqrt(D) * t),
            "w2": bf(np.random.standard_normal((E, H, H)) * 1.4 / np.sqrt(H) / t[:, None] * u),
            "w3": bf(np.random.standard_normal((E, H, D)) * 1.4 / np.sqrt(H) / u[:, None])}


def reference(x, w1, w2, w3):
    h1 = leaky_relu(f64(x) @ f64(w1))
    h2 = leaky_relu(mxq(h1, 2, "e4m3") @ mxq(f64(w2), 1, "e4m3"))
    return mxq(h2, 2, "e4m3") @ mxq(f64(w3), 1, "e4m3")

@@ -1,0 +1,231 @@
+from contextlib import ExitStack
+
+import concourse.mybir as mybir
+from concourse.masks import make_identity
+
+F32 = mybir.dt.float32
+BF16 = mybir.dt.bfloat16
+U32 = mybir.dt.uint32
+U8 = mybir.dt.uint8
+FP8X4 = mybir.dt.float8_e4m3fn_x4
+ALU = mybir.AluOpType
+ACT = mybir.ActivationFunctionType
+
+E, N, D, H = 4, 2048, 128, 512
+P = 128
+NEG_SLOPE = 0.01
+FLOPS = 2 * E * N * (D * H + H * H + H * D)
+
+JT = N // P
+GQ = 4
+QE = JT // GQ
+NQ = E * QE
+HBANKS = 6
+PINNED = True
+GREG = True
+
+
+def tile_mlpexperts_t_kernel(tc, x, w1, w2, w3, out):
+    nc = tc.nc
+    with ExitStack() as ctx:
+        const = ctx.enter_context(tc.tile_pool(name="const", bufs=1))
+        xtp = ctx.enter_context(tc.tile_pool(name="xtp", bufs=2))
+        yp = ctx.enter_context(tc.tile_pool(name="yp", bufs=8))
+        gp = ctx.enter_context(tc.tile_pool(name="gp", bufs=2))
+        qp = ctx.enter_context(tc.tile_pool(name="qp", bufs=3))
+        op = ctx.enter_context(tc.tile_pool(name="op", bufs=6))
+        ps_h = ctx.enter_context(tc.psum_pool(name="ps_h", bufs=HBANKS))
+        ps_x = ctx.enter_context(tc.psum_pool(name="ps_x", bufs=1))
+        ps_o = ctx.enter_context(tc.psum_pool(name="ps_o", bufs=1))
+        if PINNED:
+            ctx.enter_context(tc.manual_schedule())
+
+        warm_in = const.tile([P, 1], F32, name="warm_in")
+        warm_out = const.tile([P, 1], F32, name="warm_out")
+        nc.vector.memset(warm_in[:], 0.0)
+        nc.scalar.activation(out=warm_out[:], in_=warm_in[:], func=ACT.Copy, scale=NEG_SLOPE)
+
+        ident = const.tile([P, P], BF16, name="ident")
+        make_identity(nc, ident[:])
+
+        x_sb = [const.tile([P, JT, D], BF16, name="x_sb%d" % e) for e in range(E)]
+        w1_sb = const.tile([P, E, H], BF16, name="w1_sb")
+        w2_raw = [const.tile([P, 4, H], BF16, name="w2_raw%d" % e) for e in range(E)]
+        w3_raw = const.tile([P, E, 4, D], BF16, name="w3_raw")
+        w2g = [const.tile([P, H, 4], BF16, name="w2g%d" % e, align_bytes=64) for e in range(E)]
+        w3g = const.tile([P, E, D, 4], BF16, name="w3g", align_bytes=64)
+        w2q = [const.tile([P, H], U32, name="w2q%d" % e, align_bytes=64) for e in range(E)]
+        w2s = [const.tile([P, H], U8, name="w2s%d" % e, align_bytes=64) for e in range(E)]
+        w3q = const.tile([P, E * D], U32, name="w3q", align_bytes=64)
+        w3s = const.tile([P, E * D], U8, name="w3s", align_bytes=64)
+
+        x_v = [x[e].rearrange("(p j) d -> p j d", j=JT) for e in range(E)]
+        out_v = [out[e].rearrange("(p j) d -> p j d", j=JT) for e in range(E)]
+        w1_v = w1.rearrange("e d h -> d e h")
+
+        def load_w2(e):
+            nc.sync.dma_start(out=w2_raw[e][:], in_=w2[e].rearrange("(t p) m -> p t m", p=P))
+
+        nc.sync.dma_start(out=x_sb[0][:, 0:GQ, :], in_=x_v[0][:, 0:GQ, :])
+        nc.sync.dma_start(out=w1_sb[:, 0, :], in_=w1_v[:, 0, :])
+        load_w2(0)
+        nc.sync.dma_start(out=x_sb[0][:, GQ:JT, :], in_=x_v[0][:, GQ:JT, :])
+        nc.sync.dma_start(out=w3_raw[:], in_=w3.rearrange("e (t p) n -> p e t n", p=P))
+        nc.sync.dma_start(out=w1_sb[:, 1:E, :], in_=w1_v[:, 1:E, :])
+        for e in range(1, E):
+            load_w2(e)
+            nc.sync.dma_start(out=x_sb[e][:], in_=x_v[e])
+
+        def regroup(eng, dst, src):
+            if eng == "g":
+                nc.gpsimd.tensor_scalar(out=dst, in0=src.rearrange("p t c -> p c t"),
+                                        scalar1=1.0, scalar2=0.0, op0=ALU.mult, op1=ALU.add)
+            elif eng == "v":
+                nc.vector.tensor_copy(out=dst.rearrange("p (c i) t -> p c t i", i=4),
+                                      in_=src.rearrange("p t (c i) -> p c t i", i=4))
+            else:
+                nc.scalar.copy(out=dst.rearrange("p (c i) t -> p c t i", i=4),
+                               in_=src.rearrange("p t (c i) -> p c t i", i=4))
+
+        def w2_regroup(eng, e, r, pieces):
+            wd = H // pieces
+            regroup(eng, w2g[e][:, r * wd:(r + 1) * wd, :], w2_raw[e][:, :, r * wd:(r + 1) * wd])
+
+        def w3_regroup(eng, e):
+            regroup(eng, w3g[:, e], w3_raw[:, e])
+
+        def w2_quant(e):
+            nc.vector.quantize_mx(
+                out=w2q[e][:].bitcast(FP8X4), scales=w2s[e][:],
+                in_=w2g[e][:].rearrange("p m t -> p (m t)"))
+
+        def w3_quant():
+            nc.vector.quantize_mx(
+                out=w3q[:].bitcast(FP8X4), scales=w3s[:],
+                in_=w3g[:].rearrange("p e n t -> p (e n t)"))
+
+        xT = {}
+        g1 = {}
+        g2 = {}
+        h1 = {}
+        h2 = {}
+
+        def transposes(i, first, n, pool, tag):
+            e, q = divmod(i, QE)
+            if first == 0:
+                xT[i] = xtp.tile([P, GQ, P], BF16, name="xT")
+            xt_ps = pool.tile([P, n, P], BF16, name="xt_ps", tag=tag)
+            for jj in range(n):
+                nc.tensor.transpose(xt_ps[:, jj, :], x_sb[e][:, q * GQ + first + jj, :], ident[:])
+            nc.scalar.copy(out=xT[i][:, first:first + n, :], in_=xt_ps[:])
+
+        def lrelu(hb, dst):
+            perm = hb[:].rearrange("p t n -> p n t")
+            y = yp.tile([P, P, 4], BF16, name="y")
+            nc.scalar.activation(out=y[:], in_=perm, func=ACT.Copy, scale=NEG_SLOPE)
+            nc.vector.tensor_tensor(out=dst, in0=perm, in1=y[:], op=ALU.max)
+
+        def stage1(i, jj):
+            e = i // QE
+            if jj == 0:
+                g1[i] = gp.tile([P, GQ, P, 4], BF16, name="g1", align_bytes=64)
+            hb = ps_h.tile([P, 4, P], F32, name="hb")
+            for t in range(4):
+                nc.tensor.matmul(hb[:, t, :], lhsT=w1_sb[:, e, t * P:(t + 1) * P],
+                                 rhs=xT[i][:, jj, :], start=True, stop=True)
+            lrelu(hb, g1[i][:, jj])
+
+        def new_codes(tag):
+            hq = qp.tile([P, GQ * P], U32, name=tag + "q", align_bytes=64)
+            hs = qp.tile([P, GQ * P], U8, name=tag + "s", align_bytes=64)
+            return hq, hs
+
+        def quant(g, codes, first, n):
+            hq, hs = codes
+            cols = slice(first * P, (first + n) * P)
+            nc.vector.quantize_mx(out=hq[:, cols].bitcast(FP8X4), scales=hs[:, cols],
+                                  in_=g[:, first:first + n].rearrange("p j n t -> p (j n t)"))
+
+        def stage2(i, jj):
+            e = i // QE
+            if jj == 0:
+                g2[i] = gp.tile([P, GQ, P, 4], BF16, name="g2", align_bytes=64)
+            hq, hs = h1[i]
+            cols = slice(jj * P, (jj + 1) * P)
+            hb = ps_h.tile([P, 4, P], F32, name="hb")
+            for c in range(4):
+                wc = slice(c * P, (c + 1) * P)
+                nc.tensor.matmul_mx(out=hb[:, c, :],
+                                    lhsT=w2q[e][:, wc].bitcast(FP8X4), lhsT_scale=w2s[e][:, wc],
+                                    rhs=hq[:, cols].bitcast(FP8X4), rhs_scale=hs[:, cols],
+                                    start=True, stop=True)
+            lrelu(hb, g2[i][:, jj])
+
+        def stage3(i, first, n, pool, tag):
+            e, q = divmod(i, QE)
+            hq, hs = h2[i]
+            wc = slice(e * D, (e + 1) * D)
+            o_ps = pool.tile([P, n, D], F32, name="o_ps", tag=tag)
+            for jj in range(n):
+                cols = slice((first + jj) * P, (first + jj + 1) * P)
+                nc.tensor.matmul_mx(out=o_ps[:, jj, :],
+                                    lhsT=hq[:, cols].bitcast(FP8X4), lhsT_scale=hs[:, cols],
+                                    rhs=w3q[:, wc].bitcast(FP8X4), rhs_scale=w3s[:, wc],
+                                    start=True, stop=True)
+            o_sb = op.tile([P, n, D], F32, name="o_sb")
+            nc.scalar.copy(out=o_sb[:], in_=o_ps[:])
+            j0 = q * GQ + first
+            nc.sync.dma_start(out=out_v[e][:, j0:j0 + n, :], in_=o_sb[:])
+
+        if GREG:
+            for r in range(4):
+                w2_regroup("g", 0, r, 4)
+            for e in range(E):
+                w3_regroup("g", e)
+            for e in range(1, E):
+                for r in range(4):
+                    w2_regroup("g", e, r, 4)
+        transposes(0, 0, 1, ps_h, "hb")
+        transposes(0, 1, GQ - 1, ps_h, "hb")
+        if not GREG:
+            w2_regroup("v", 0, 0, 1)
+        for i in range(NQ + 1):
+            nxt = (i + 2) // QE
+            pieces = (not GREG) and 1 <= nxt < E and (i + 2) % QE < 2
+            half = ((i + 2) % QE) * 2
+            for jj in range(GQ):
+                if i < NQ:
+                    stage1(i, jj)
+                if jj == 0 and 0 <= i - 2:
+                    h2[i - 2] = new_codes("h2")
+                    quant(g2[i - 2], h2[i - 2], 0, GQ)
+                if jj == 1 and i == 1 and not GREG:
+                    for e in range(E):
+                        w3_regroup("v", e)
+                if jj == 1 and i == 2:
+                    w3_quant()
+                if jj == 2 and (i + 1) % QE == 0 and i + 1 < NQ:
+                    w2_quant((i + 1) // QE)
+            if i + 1 < NQ:
+                transposes(i + 1, 0, GQ, ps_x, "xt_ps")
+            if pieces:
+                w2_regroup("s", nxt, half, 4)
+            for jj in range(GQ):
+                if 0 <= i - 1:
+                    stage2(i - 1, jj)
+                if jj == 0 and i < NQ:
+                    h1[i] = new_codes("h1")
+                    quant(g1[i], h1[i], 0, GQ)
+                if jj == 0 and i == 0:
+                    w2_quant(0)
+                if i == NQ and jj == 1:
+                    h2[NQ - 1] = new_codes("h2")
+                if i == NQ and jj >= 1:
+                    quant(g2[NQ - 1], h2[NQ - 1], jj - 1, 1)
+            if 0 <= i - 2:
+                stage3(i - 2, 0, GQ, ps_o, "o_ps")
+            if pieces:
+                w2_regroup("s", nxt, half + 1, 4)
+        quant(g2[NQ - 1], h2[NQ - 1], GQ - 1, 1)
+        for jj in range(GQ):
+            stage3(NQ - 1, jj, 1, ps_h, "hb")

@@ -23,6 +23,7 @@ NQ = E * QE
 HBANKS = 6
 PINNED = True
 GREG = True
+SHIFT_EVERY = 12
 
 
 def tile_mlpexperts_t_kernel(tc, x, w1, w2, w3, out):
@@ -119,11 +120,23 @@ def tile_mlpexperts_t_kernel(tc, x, w1, w2, w3, out):
                 nc.tensor.transpose(xt_ps[:, jj, :], x_sb[e][:, q * GQ + first + jj, :], ident[:])
             nc.scalar.copy(out=xT[i][:, first:first + n, :], in_=xt_ps[:])
 
+        banks = [0]
+
         def lrelu(hb, dst):
             perm = hb[:].rearrange("p t n -> p n t")
-            y = yp.tile([P, P, 4], BF16, name="y")
-            nc.scalar.activation(out=y[:], in_=perm, func=ACT.Copy, scale=NEG_SLOPE)
-            nc.vector.tensor_tensor(out=dst, in0=perm, in1=y[:], op=ALU.max)
+            k = banks[0]
+            banks[0] = k + 1
+            a = yp.tile([P, P, 4], BF16, name="y")
+            nc.scalar.copy(out=a[:], in_=perm)
+            if k % SHIFT_EVERY == SHIFT_EVERY - 5:
+                y = yp.tile([P, P, 4], BF16, name="y")
+                nc.scalar.activation(out=y[:], in_=perm, func=ACT.Copy, scale=NEG_SLOPE)
+                nc.vector.tensor_tensor(out=dst.rearrange("p n t -> p (n t)"),
+                                        in0=a[:].rearrange("p n t -> p (n t)"),
+                                        in1=y[:].rearrange("p n t -> p (n t)"), op=ALU.max)
+            else:
+                nc.vector.scalar_tensor_tensor(out=dst, in0=perm, scalar=NEG_SLOPE, in1=a[:],
+                                               op0=ALU.mult, op1=ALU.max)
 
         def stage1(i, jj):
             e = i // QE
@@ -186,7 +199,6 @@ def tile_mlpexperts_t_kernel(tc, x, w1, w2, w3, out):
                 for r in range(4):
                     w2_regroup("g", e, r, 4)
         transposes(0, 0, 1, ps_h, "hb")
-        transposes(0, 1, GQ - 1, ps_h, "hb")
         if not GREG:
             w2_regroup("v", 0, 0, 1)
         for i in range(NQ + 1):
@@ -196,6 +208,8 @@ def tile_mlpexperts_t_kernel(tc, x, w1, w2, w3, out):
             for jj in range(GQ):
                 if i < NQ:
                     stage1(i, jj)
+                if jj == 0 and i == 0:
+                    transposes(0, 1, GQ - 1, ps_h, "hb")
                 if jj == 0 and 0 <= i - 2:
                     h2[i - 2] = new_codes("h2")
                     quant(g2[i - 2], h2[i - 2], 0, GQ)

@@ -126,17 +126,16 @@ def tile_mlpexperts_t_kernel(tc, x, w1, w2, w3, out):
             perm = hb[:].rearrange("p t n -> p n t")
             k = banks[0]
             banks[0] = k + 1
-            a = yp.tile([P, P, 4], BF16, name="y")
-            nc.scalar.copy(out=a[:], in_=perm)
+            y = yp.tile([P, P, 4], BF16, name="y")
+            nc.scalar.activation(out=y[:], in_=perm, func=ACT.Copy, scale=NEG_SLOPE)
             if k % SHIFT_EVERY == SHIFT_EVERY - 5:
-                y = yp.tile([P, P, 4], BF16, name="y")
-                nc.scalar.activation(out=y[:], in_=perm, func=ACT.Copy, scale=NEG_SLOPE)
+                a = yp.tile([P, P, 4], BF16, name="y")
+                nc.scalar.copy(out=a[:], in_=perm)
                 nc.vector.tensor_tensor(out=dst.rearrange("p n t -> p (n t)"),
                                         in0=a[:].rearrange("p n t -> p (n t)"),
                                         in1=y[:].rearrange("p n t -> p (n t)"), op=ALU.max)
             else:
-                nc.vector.scalar_tensor_tensor(out=dst, in0=perm, scalar=NEG_SLOPE, in1=a[:],
-                                               op0=ALU.mult, op1=ALU.max)
+                nc.vector.tensor_tensor(out=dst, in0=perm, in1=y[:], op=ALU.max)
 
         def stage1(i, jj):
             e = i // QE

@@ -23,7 +23,7 @@ NQ = E * QE
 HBANKS = 6
 PINNED = True
 GREG = True
-SHIFT_EVERY = 12
+SHIFT_EVERY = 100000
 
 
 def tile_mlpexperts_t_kernel(tc, x, w1, w2, w3, out):
@@ -126,16 +126,17 @@ def tile_mlpexperts_t_kernel(tc, x, w1, w2, w3, out):
             perm = hb[:].rearrange("p t n -> p n t")
             k = banks[0]
             banks[0] = k + 1
-            y = yp.tile([P, P, 4], BF16, name="y")
-            nc.scalar.activation(out=y[:], in_=perm, func=ACT.Copy, scale=NEG_SLOPE)
+            a = yp.tile([P, P, 4], BF16, name="y")
+            nc.scalar.copy(out=a[:], in_=perm)
             if k % SHIFT_EVERY == SHIFT_EVERY - 5:
-                a = yp.tile([P, P, 4], BF16, name="y")
-                nc.scalar.copy(out=a[:], in_=perm)
+                y = yp.tile([P, P, 4], BF16, name="y")
+                nc.scalar.activation(out=y[:], in_=perm, func=ACT.Copy, scale=NEG_SLOPE)
                 nc.vector.tensor_tensor(out=dst.rearrange("p n t -> p (n t)"),
                                         in0=a[:].rearrange("p n t -> p (n t)"),
                                         in1=y[:].rearrange("p n t -> p (n t)"), op=ALU.max)
             else:
-                nc.vector.tensor_tensor(out=dst, in0=perm, in1=y[:], op=ALU.max)
+                nc.vector.scalar_tensor_tensor(out=dst, in0=perm, scalar=NEG_SLOPE, in1=a[:],
+                                               op0=ALU.mult, op1=ALU.max)
 
         def stage1(i, jj):
             e = i // QE

@@ -23,7 +23,7 @@ NQ = E * QE
 HBANKS = 6
 PINNED = True
 GREG = True
-SHIFT_EVERY = 100000
+SHIFT_EVERY = 12
 
 
 def tile_mlpexperts_t_kernel(tc, x, w1, w2, w3, out):
@@ -128,7 +128,7 @@ def tile_mlpexperts_t_kernel(tc, x, w1, w2, w3, out):
             banks[0] = k + 1
             a = yp.tile([P, P, 4], BF16, name="y")
             nc.scalar.copy(out=a[:], in_=perm)
-            if k % SHIFT_EVERY == SHIFT_EVERY - 5:
+            if k % SHIFT_EVERY == SHIFT_EVERY // 2:
                 y = yp.tile([P, P, 4], BF16, name="y")
                 nc.scalar.activation(out=y[:], in_=perm, func=ACT.Copy, scale=NEG_SLOPE)
                 nc.vector.tensor_tensor(out=dst.rearrange("p n t -> p (n t)"),
@@ -199,6 +199,7 @@ def tile_mlpexperts_t_kernel(tc, x, w1, w2, w3, out):
                 for r in range(4):
                     w2_regroup("g", e, r, 4)
         transposes(0, 0, 1, ps_h, "hb")
+        transposes(0, 1, GQ - 1, ps_h, "hb")
         if not GREG:
             w2_regroup("v", 0, 0, 1)
         for i in range(NQ + 1):
@@ -208,8 +209,6 @@ def tile_mlpexperts_t_kernel(tc, x, w1, w2, w3, out):
             for jj in range(GQ):
                 if i < NQ:
                     stage1(i, jj)
-                if jj == 0 and i == 0:
-                    transposes(0, 1, GQ - 1, ps_h, "hb")
                 if jj == 0 and 0 <= i - 2:
                     h2[i - 2] = new_codes("h2")
                     quant(g2[i - 2], h2[i - 2], 0, GQ)

@@ -23,7 +23,7 @@ NQ = E * QE
 HBANKS = 6
 PINNED = True
 GREG = True
-SHIFT_EVERY = 12
+SHIFT_EVERY = 14
 
 
 def tile_mlpexperts_t_kernel(tc, x, w1, w2, w3, out):

@@ -13,33 +13,34 @@ ACT = mybir.ActivationFunctionType
 
 E, N, D, H = 4, 2048, 128, 512
 P = 128
+PACK = 4
 NEG_SLOPE = 0.01
+F32_MAX = 3.4028234663852886e38
 FLOPS = 2 * E * N * (D * H + H * H + H * D)
 
-JT = N // P
+GROUPS = N // P
 GQ = 4
-QE = JT // GQ
+QE = GROUPS // GQ
 NQ = E * QE
-HBANKS = 6
-PINNED = True
-GREG = True
-SHIFT_EVERY = 14
+H_BANKS = 6
+G_FIRST = 4
+OC_ON_VECTOR = ()
 
 
 def tile_mlpexperts_t_kernel(tc, x, w1, w2, w3, out):
     nc = tc.nc
     with ExitStack() as ctx:
         const = ctx.enter_context(tc.tile_pool(name="const", bufs=1))
-        xtp = ctx.enter_context(tc.tile_pool(name="xtp", bufs=2))
-        yp = ctx.enter_context(tc.tile_pool(name="yp", bufs=8))
-        gp = ctx.enter_context(tc.tile_pool(name="gp", bufs=2))
-        qp = ctx.enter_context(tc.tile_pool(name="qp", bufs=3))
-        op = ctx.enter_context(tc.tile_pool(name="op", bufs=6))
-        ps_h = ctx.enter_context(tc.psum_pool(name="ps_h", bufs=HBANKS))
+        xt_pool = ctx.enter_context(tc.tile_pool(name="xtp", bufs=2))
+        cast_pool = ctx.enter_context(tc.tile_pool(name="yp", bufs=8))
+        f32_pool = ctx.enter_context(tc.tile_pool(name="vp", bufs=2))
+        grouped_pool = ctx.enter_context(tc.tile_pool(name="gp", bufs=2))
+        codes_pool = ctx.enter_context(tc.tile_pool(name="qp", bufs=3))
+        out_pool = ctx.enter_context(tc.tile_pool(name="op", bufs=6))
+        ps_h = ctx.enter_context(tc.psum_pool(name="ps_h", bufs=H_BANKS))
         ps_x = ctx.enter_context(tc.psum_pool(name="ps_x", bufs=1))
         ps_o = ctx.enter_context(tc.psum_pool(name="ps_o", bufs=1))
-        if PINNED:
-            ctx.enter_context(tc.manual_schedule())
+        ctx.enter_context(tc.manual_schedule())
 
         warm_in = const.tile([P, 1], F32, name="warm_in")
         warm_out = const.tile([P, 1], F32, name="warm_out")
@@ -49,196 +50,194 @@ def tile_mlpexperts_t_kernel(tc, x, w1, w2, w3, out):
         ident = const.tile([P, P], BF16, name="ident")
         make_identity(nc, ident[:])
 
-        x_sb = [const.tile([P, JT, D], BF16, name="x_sb%d" % e) for e in range(E)]
+        x_sb = [const.tile([P, GROUPS, D], BF16, name="x_sb%d" % e) for e in range(E)]
         w1_sb = const.tile([P, E, H], BF16, name="w1_sb")
-        w2_raw = [const.tile([P, 4, H], BF16, name="w2_raw%d" % e) for e in range(E)]
-        w3_raw = const.tile([P, E, 4, D], BF16, name="w3_raw")
-        w2g = [const.tile([P, H, 4], BF16, name="w2g%d" % e, align_bytes=64) for e in range(E)]
-        w3g = const.tile([P, E, D, 4], BF16, name="w3g", align_bytes=64)
-        w2q = [const.tile([P, H], U32, name="w2q%d" % e, align_bytes=64) for e in range(E)]
-        w2s = [const.tile([P, H], U8, name="w2s%d" % e, align_bytes=64) for e in range(E)]
-        w3q = const.tile([P, E * D], U32, name="w3q", align_bytes=64)
-        w3s = const.tile([P, E * D], U8, name="w3s", align_bytes=64)
+        w2_raw = [const.tile([P, PACK, H], BF16, name="w2_raw%d" % e) for e in range(E)]
+        w3_raw = const.tile([P, E, PACK, D], BF16, name="w3_raw")
+        w2_grouped = [const.tile([P, H, PACK], BF16, name="w2g%d" % e, align_bytes=64)
+                      for e in range(E)]
+        w3_grouped = const.tile([P, E, D, PACK], BF16, name="w3g", align_bytes=64)
+        w2_words = [const.tile([P, H], U32, name="w2q%d" % e, align_bytes=64) for e in range(E)]
+        w2_scales = [const.tile([P, H], U8, name="w2s%d" % e, align_bytes=64) for e in range(E)]
+        w3_words = const.tile([P, E * D], U32, name="w3q", align_bytes=64)
+        w3_scales = const.tile([P, E * D], U8, name="w3s", align_bytes=64)
 
-        x_v = [x[e].rearrange("(p j) d -> p j d", j=JT) for e in range(E)]
-        out_v = [out[e].rearrange("(p j) d -> p j d", j=JT) for e in range(E)]
-        w1_v = w1.rearrange("e d h -> d e h")
+        x_view = [x[e].rearrange("(p j) d -> p j d", j=GROUPS) for e in range(E)]
+        out_view = [out[e].rearrange("(p j) d -> p j d", j=GROUPS) for e in range(E)]
+        w1_view = w1.rearrange("e d h -> d e h")
 
         def load_w2(e):
             nc.sync.dma_start(out=w2_raw[e][:], in_=w2[e].rearrange("(t p) m -> p t m", p=P))
 
-        nc.sync.dma_start(out=x_sb[0][:, 0:GQ, :], in_=x_v[0][:, 0:GQ, :])
-        nc.sync.dma_start(out=w1_sb[:, 0, :], in_=w1_v[:, 0, :])
+        nc.sync.dma_start(out=x_sb[0][:, 0:GQ, :], in_=x_view[0][:, 0:GQ, :])
+        nc.sync.dma_start(out=w1_sb[:, 0, :], in_=w1_view[:, 0, :])
         load_w2(0)
-        nc.sync.dma_start(out=x_sb[0][:, GQ:JT, :], in_=x_v[0][:, GQ:JT, :])
+        nc.sync.dma_start(out=x_sb[0][:, GQ:GROUPS, :], in_=x_view[0][:, GQ:GROUPS, :])
         nc.sync.dma_start(out=w3_raw[:], in_=w3.rearrange("e (t p) n -> p e t n", p=P))
-        nc.sync.dma_start(out=w1_sb[:, 1:E, :], in_=w1_v[:, 1:E, :])
+        nc.sync.dma_start(out=w1_sb[:, 1:E, :], in_=w1_view[:, 1:E, :])
         for e in range(1, E):
             load_w2(e)
-            nc.sync.dma_start(out=x_sb[e][:], in_=x_v[e])
+            nc.sync.dma_start(out=x_sb[e][:], in_=x_view[e])
 
-        def regroup(eng, dst, src):
-            if eng == "g":
-                nc.gpsimd.tensor_scalar(out=dst, in0=src.rearrange("p t c -> p c t"),
-                                        scalar1=1.0, scalar2=0.0, op0=ALU.mult, op1=ALU.add)
-            elif eng == "v":
-                nc.vector.tensor_copy(out=dst.rearrange("p (c i) t -> p c t i", i=4),
-                                      in_=src.rearrange("p t (c i) -> p c t i", i=4))
-            else:
-                nc.scalar.copy(out=dst.rearrange("p (c i) t -> p c t i", i=4),
-                               in_=src.rearrange("p t (c i) -> p c t i", i=4))
+        def regroup(dst, src):
+            nc.gpsimd.tensor_scalar(out=dst, in0=src.rearrange("p t c -> p c t"),
+                                    scalar1=1.0, scalar2=0.0, op0=ALU.mult, op1=ALU.add)
 
-        def w2_regroup(eng, e, r, pieces):
-            wd = H // pieces
-            regroup(eng, w2g[e][:, r * wd:(r + 1) * wd, :], w2_raw[e][:, :, r * wd:(r + 1) * wd])
+        def regroup_w2(e):
+            for c in range(PACK):
+                cols = slice(c * P, (c + 1) * P)
+                regroup(w2_grouped[e][:, cols, :], w2_raw[e][:, :, cols])
 
-        def w3_regroup(eng, e):
-            regroup(eng, w3g[:, e], w3_raw[:, e])
+        def quantise_w2(e):
+            nc.vector.quantize_mx(out=w2_words[e][:].bitcast(FP8X4), scales=w2_scales[e][:],
+                                  in_=w2_grouped[e][:].rearrange("p m t -> p (m t)"))
 
-        def w2_quant(e):
-            nc.vector.quantize_mx(
-                out=w2q[e][:].bitcast(FP8X4), scales=w2s[e][:],
-                in_=w2g[e][:].rearrange("p m t -> p (m t)"))
+        def quantise_w3():
+            nc.vector.quantize_mx(out=w3_words[:].bitcast(FP8X4), scales=w3_scales[:],
+                                  in_=w3_grouped[:].rearrange("p e n t -> p (e n t)"))
 
-        def w3_quant():
-            nc.vector.quantize_mx(
-                out=w3q[:].bitcast(FP8X4), scales=w3s[:],
-                in_=w3g[:].rearrange("p e n t -> p (e n t)"))
+        x_t = {}
+        grouped = {}
+        codes = {}
+        f32_copy = {}
 
-        xT = {}
-        g1 = {}
-        g2 = {}
-        h1 = {}
-        h2 = {}
+        def grouped_of(step):
+            if step not in grouped:
+                grouped[step] = grouped_pool.tile([P, 2, GQ, P, PACK], BF16, name="gg",
+                                                  align_bytes=64)
+            return grouped[step]
 
-        def transposes(i, first, n, pool, tag):
-            e, q = divmod(i, QE)
+        def codes_of(step):
+            if step not in codes:
+                words = codes_pool.tile([P, 2 * GQ * P], U32, name="hq", align_bytes=64)
+                scales = codes_pool.tile([P, 2 * GQ * P], U8, name="hs", align_bytes=64)
+                codes[step] = (words, scales)
+            return codes[step]
+
+        def transpose_x(quad, first, n, pool, tag):
+            e, q = divmod(quad, QE)
             if first == 0:
-                xT[i] = xtp.tile([P, GQ, P], BF16, name="xT")
+                x_t[quad] = xt_pool.tile([P, GQ, P], BF16, name="xT")
             xt_ps = pool.tile([P, n, P], BF16, name="xt_ps", tag=tag)
-            for jj in range(n):
-                nc.tensor.transpose(xt_ps[:, jj, :], x_sb[e][:, q * GQ + first + jj, :], ident[:])
-            nc.scalar.copy(out=xT[i][:, first:first + n, :], in_=xt_ps[:])
+            for g in range(n):
+                nc.tensor.transpose(xt_ps[:, g, :], x_sb[e][:, q * GQ + first + g, :], ident[:])
+            nc.scalar.copy(out=x_t[quad][:, first:first + n, :], in_=xt_ps[:])
 
-        banks = [0]
+        def lrelu(bank, dst):
+            v = bank[:].rearrange("p t n -> p n t")
+            cast = cast_pool.tile([P, P, PACK], BF16, name="y")
+            nc.scalar.copy(out=cast[:], in_=v)
+            nc.vector.scalar_tensor_tensor(out=dst, in0=v, scalar=NEG_SLOPE, in1=cast[:],
+                                           op0=ALU.mult, op1=ALU.max)
 
-        def lrelu(hb, dst):
-            perm = hb[:].rearrange("p t n -> p n t")
-            k = banks[0]
-            banks[0] = k + 1
-            a = yp.tile([P, P, 4], BF16, name="y")
-            nc.scalar.copy(out=a[:], in_=perm)
-            if k % SHIFT_EVERY == SHIFT_EVERY // 2:
-                y = yp.tile([P, P, 4], BF16, name="y")
-                nc.scalar.activation(out=y[:], in_=perm, func=ACT.Copy, scale=NEG_SLOPE)
-                nc.vector.tensor_tensor(out=dst.rearrange("p n t -> p (n t)"),
-                                        in0=a[:].rearrange("p n t -> p (n t)"),
-                                        in1=y[:].rearrange("p n t -> p (n t)"), op=ALU.max)
+        def layer1(quad, g):
+            e = quad // QE
+            bank = ps_h.tile([P, PACK, P], F32, name="hb")
+            for t in range(PACK):
+                nc.tensor.matmul(bank[:, t, :], lhsT=w1_sb[:, e, t * P:(t + 1) * P],
+                                 rhs=x_t[quad][:, g, :], start=True, stop=True)
+            if g == 0 and quad >= G_FIRST:
+                f32_copy[quad] = f32_pool.tile([P, P * PACK], F32, name="vs")
+                nc.scalar.copy(out=f32_copy[quad][:].rearrange("p (n t) -> p n t", t=PACK),
+                               in_=bank[:].rearrange("p t n -> p n t"))
             else:
-                nc.vector.scalar_tensor_tensor(out=dst, in0=perm, scalar=NEG_SLOPE, in1=a[:],
-                                               op0=ALU.mult, op1=ALU.max)
+                lrelu(bank, grouped_of(quad)[:, 0, g])
 
-        def stage1(i, jj):
-            e = i // QE
-            if jj == 0:
-                g1[i] = gp.tile([P, GQ, P, 4], BF16, name="g1", align_bytes=64)
-            hb = ps_h.tile([P, 4, P], F32, name="hb")
-            for t in range(4):
-                nc.tensor.matmul(hb[:, t, :], lhsT=w1_sb[:, e, t * P:(t + 1) * P],
-                                 rhs=xT[i][:, jj, :], start=True, stop=True)
-            lrelu(hb, g1[i][:, jj])
+        def lrelu_on_gpsimd(quad):
+            nc.gpsimd.memset(grouped[quad - 1][:, 0, 0, 0, 0:2], 0.0)
+            v = f32_copy[quad]
+            m1 = f32_pool.tile([P, P * PACK], F32, name="m1")
+            nc.gpsimd.tensor_scalar(out=m1[:], in0=v[:], scalar1=NEG_SLOPE - 1.0, scalar2=0.0,
+                                    op0=ALU.mult, op1=ALU.add)
+            m2 = f32_pool.tile([P, P * PACK], F32, name="m2")
+            nc.gpsimd.tensor_scalar(out=m2[:], in0=m1[:], scalar1=F32_MAX, scalar2=0.0,
+                                    op0=ALU.min, op1=ALU.max)
+            nc.gpsimd.tensor_tensor(out=grouped_of(quad)[:, 0, 0].rearrange("p n t -> p (n t)"),
+                                    in0=v[:], in1=m2[:], op=ALU.add)
 
-        def new_codes(tag):
-            hq = qp.tile([P, GQ * P], U32, name=tag + "q", align_bytes=64)
-            hs = qp.tile([P, GQ * P], U8, name=tag + "s", align_bytes=64)
-            return hq, hs
+        def quantise(step, lo, hi):
+            words, scales = codes_of(step)
+            cols = slice(lo * P, hi * P)
+            src = grouped[step][:].rearrange("p s j n t -> p (s j) (n t)")
+            nc.vector.quantize_mx(out=words[:, cols].bitcast(FP8X4), scales=scales[:, cols],
+                                  in_=src[:, lo:hi, :].rearrange("p j c -> p (j c)"))
 
-        def quant(g, codes, first, n):
-            hq, hs = codes
-            cols = slice(first * P, (first + n) * P)
-            nc.vector.quantize_mx(out=hq[:, cols].bitcast(FP8X4), scales=hs[:, cols],
-                                  in_=g[:, first:first + n].rearrange("p j n t -> p (j n t)"))
-
-        def stage2(i, jj):
-            e = i // QE
-            if jj == 0:
-                g2[i] = gp.tile([P, GQ, P, 4], BF16, name="g2", align_bytes=64)
-            hq, hs = h1[i]
-            cols = slice(jj * P, (jj + 1) * P)
-            hb = ps_h.tile([P, 4, P], F32, name="hb")
-            for c in range(4):
-                wc = slice(c * P, (c + 1) * P)
-                nc.tensor.matmul_mx(out=hb[:, c, :],
-                                    lhsT=w2q[e][:, wc].bitcast(FP8X4), lhsT_scale=w2s[e][:, wc],
-                                    rhs=hq[:, cols].bitcast(FP8X4), rhs_scale=hs[:, cols],
+        def layer2(quad, g):
+            e = quad // QE
+            words, scales = codes[quad]
+            tokens = slice(g * P, (g + 1) * P)
+            bank = ps_h.tile([P, PACK, P], F32, name="hb")
+            for t in range(PACK):
+                chunk = slice(t * P, (t + 1) * P)
+                nc.tensor.matmul_mx(out=bank[:, t, :],
+                                    lhsT=w2_words[e][:, chunk].bitcast(FP8X4),
+                                    lhsT_scale=w2_scales[e][:, chunk],
+                                    rhs=words[:, tokens].bitcast(FP8X4),
+                                    rhs_scale=scales[:, tokens],
                                     start=True, stop=True)
-            lrelu(hb, g2[i][:, jj])
+            lrelu(bank, grouped_of(quad + 2)[:, 1, g])
 
-        def stage3(i, first, n, pool, tag):
-            e, q = divmod(i, QE)
-            hq, hs = h2[i]
-            wc = slice(e * D, (e + 1) * D)
+        def layer3(quad, first, n, pool, tag):
+            e, q = divmod(quad, QE)
+            words, scales = codes[quad + 2]
+            w_cols = slice(e * D, (e + 1) * D)
             o_ps = pool.tile([P, n, D], F32, name="o_ps", tag=tag)
-            for jj in range(n):
-                cols = slice((first + jj) * P, (first + jj + 1) * P)
-                nc.tensor.matmul_mx(out=o_ps[:, jj, :],
-                                    lhsT=hq[:, cols].bitcast(FP8X4), lhsT_scale=hs[:, cols],
-                                    rhs=w3q[:, wc].bitcast(FP8X4), rhs_scale=w3s[:, wc],
+            for g in range(n):
+                tokens = slice((GQ + first + g) * P, (GQ + first + g + 1) * P)
+                nc.tensor.matmul_mx(out=o_ps[:, g, :],
+                                    lhsT=words[:, tokens].bitcast(FP8X4),
+                                    lhsT_scale=scales[:, tokens],
+                                    rhs=w3_words[:, w_cols].bitcast(FP8X4),
+                                    rhs_scale=w3_scales[:, w_cols],
                                     start=True, stop=True)
-            o_sb = op.tile([P, n, D], F32, name="o_sb")
-            nc.scalar.copy(out=o_sb[:], in_=o_ps[:])
+            o_sb = out_pool.tile([P, n, D], F32, name="o_sb")
+            if quad in OC_ON_VECTOR:
+                nc.vector.tensor_copy(out=o_sb[:], in_=o_ps[:])
+            else:
+                nc.scalar.copy(out=o_sb[:], in_=o_ps[:])
             j0 = q * GQ + first
-            nc.sync.dma_start(out=out_v[e][:, j0:j0 + n, :], in_=o_sb[:])
+            nc.sync.dma_start(out=out_view[e][:, j0:j0 + n, :], in_=o_sb[:])
 
-        if GREG:
-            for r in range(4):
-                w2_regroup("g", 0, r, 4)
-            for e in range(E):
-                w3_regroup("g", e)
-            for e in range(1, E):
-                for r in range(4):
-                    w2_regroup("g", e, r, 4)
-        transposes(0, 0, 1, ps_h, "hb")
-        transposes(0, 1, GQ - 1, ps_h, "hb")
-        if not GREG:
-            w2_regroup("v", 0, 0, 1)
-        for i in range(NQ + 1):
-            nxt = (i + 2) // QE
-            pieces = (not GREG) and 1 <= nxt < E and (i + 2) % QE < 2
-            half = ((i + 2) % QE) * 2
-            for jj in range(GQ):
-                if i < NQ:
-                    stage1(i, jj)
-                if jj == 0 and 0 <= i - 2:
-                    h2[i - 2] = new_codes("h2")
-                    quant(g2[i - 2], h2[i - 2], 0, GQ)
-                if jj == 1 and i == 1 and not GREG:
-                    for e in range(E):
-                        w3_regroup("v", e)
-                if jj == 1 and i == 2:
-                    w3_quant()
-                if jj == 2 and (i + 1) % QE == 0 and i + 1 < NQ:
-                    w2_quant((i + 1) // QE)
-            if i + 1 < NQ:
-                transposes(i + 1, 0, GQ, ps_x, "xt_ps")
-            if pieces:
-                w2_regroup("s", nxt, half, 4)
-            for jj in range(GQ):
-                if 0 <= i - 1:
-                    stage2(i - 1, jj)
-                if jj == 0 and i < NQ:
-                    h1[i] = new_codes("h1")
-                    quant(g1[i], h1[i], 0, GQ)
-                if jj == 0 and i == 0:
-                    w2_quant(0)
-                if i == NQ and jj == 1:
-                    h2[NQ - 1] = new_codes("h2")
-                if i == NQ and jj >= 1:
-                    quant(g2[NQ - 1], h2[NQ - 1], jj - 1, 1)
+        regroup_w2(0)
+        for e in range(E):
+            regroup(w3_grouped[:, e], w3_raw[:, e])
+        for e in range(1, E):
+            regroup_w2(e)
+
+        transpose_x(0, 0, 1, ps_h, "hb")
+        transpose_x(0, 1, GQ - 1, ps_h, "hb")
+
+        LAST = NQ + 1
+        for i in range(LAST + 1):
+            units = []
+            if i < NQ:
+                units.extend([(1, i, g) for g in range(GQ)])
             if 0 <= i - 2:
-                stage3(i - 2, 0, GQ, ps_o, "o_ps")
-            if pieces:
-                w2_regroup("s", nxt, half + 1, 4)
-        quant(g2[NQ - 1], h2[NQ - 1], GQ - 1, 1)
-        for jj in range(GQ):
-            stage3(NQ - 1, jj, 1, ps_h, "hb")
+                units.extend([(2, i - 2, g) for g in range(GQ)])
+            for k, (layer, quad, g) in enumerate(units):
+                if layer == 1:
+                    layer1(quad, g)
+                else:
+                    layer2(quad, g)
+                if k == 1:
+                    if i == 1:
+                        quantise_w2(0)
+                    if i == 3:
+                        quantise_w3()
+                    if i % QE == 0 and 0 < i < NQ:
+                        quantise_w2(i // QE)
+                    if i >= 1:
+                        lo = 0 if i - 1 < NQ else GQ
+                        hi = 2 * GQ if i - 3 >= 0 else GQ
+                        quantise(i - 1, lo, hi)
+                    if G_FIRST <= i < NQ:
+                        lrelu_on_gpsimd(i)
+                if layer == 1 and g == GQ - 1 and i + 1 < NQ:
+                    transpose_x(i + 1, 0, GQ, ps_x, "xt_ps")
+                if i == LAST and k >= 1:
+                    quantise(LAST, GQ + k - 1, GQ + k)
+            if 0 <= i - 3:
+                layer3(i - 3, 0, GQ, ps_o, "o_ps")
+        quantise(LAST, 2 * GQ - 1, 2 * GQ)
+        for g in range(GQ):
+            layer3(NQ - 1, g, 1, ps_h, "hb")

@@ -24,6 +24,7 @@ QE = GROUPS // GQ
 NQ = E * QE
 H_BANKS = 6
 G_FIRST = 4
+G_TOKENS = 96
 OC_ON_VECTOR = ()
 
 
@@ -123,12 +124,12 @@ def tile_mlpexperts_t_kernel(tc, x, w1, w2, w3, out):
                 nc.tensor.transpose(xt_ps[:, g, :], x_sb[e][:, q * GQ + first + g, :], ident[:])
             nc.scalar.copy(out=x_t[quad][:, first:first + n, :], in_=xt_ps[:])
 
-        def lrelu(bank, dst):
-            v = bank[:].rearrange("p t n -> p n t")
-            cast = cast_pool.tile([P, P, PACK], BF16, name="y")
+        def lrelu(bank, dst, first=0):
+            v = bank[:].rearrange("p t n -> p n t")[:, first:P, :]
+            cast = cast_pool.tile([P, P - first, PACK], BF16, name="y")
             nc.scalar.copy(out=cast[:], in_=v)
-            nc.vector.scalar_tensor_tensor(out=dst, in0=v, scalar=NEG_SLOPE, in1=cast[:],
-                                           op0=ALU.mult, op1=ALU.max)
+            nc.vector.scalar_tensor_tensor(out=dst[:, first:P, :], in0=v, scalar=NEG_SLOPE,
+                                           in1=cast[:], op0=ALU.mult, op1=ALU.max)
 
         def layer1(quad, g):
             e = quad // QE
@@ -137,22 +138,24 @@ def tile_mlpexperts_t_kernel(tc, x, w1, w2, w3, out):
                 nc.tensor.matmul(bank[:, t, :], lhsT=w1_sb[:, e, t * P:(t + 1) * P],
                                  rhs=x_t[quad][:, g, :], start=True, stop=True)
             if g == 0 and quad >= G_FIRST:
-                f32_copy[quad] = f32_pool.tile([P, P * PACK], F32, name="vs")
+                f32_copy[quad] = f32_pool.tile([P, G_TOKENS * PACK], F32, name="vs")
                 nc.scalar.copy(out=f32_copy[quad][:].rearrange("p (n t) -> p n t", t=PACK),
-                               in_=bank[:].rearrange("p t n -> p n t"))
+                               in_=bank[:].rearrange("p t n -> p n t")[:, 0:G_TOKENS, :])
+                lrelu(bank, grouped_of(quad)[:, 0, g], G_TOKENS)
             else:
                 lrelu(bank, grouped_of(quad)[:, 0, g])
 
         def lrelu_on_gpsimd(quad):
             nc.gpsimd.memset(grouped[quad - 1][:, 0, 0, 0, 0:2], 0.0)
             v = f32_copy[quad]
-            m1 = f32_pool.tile([P, P * PACK], F32, name="m1")
+            m1 = f32_pool.tile([P, G_TOKENS * PACK], F32, name="m1")
             nc.gpsimd.tensor_scalar(out=m1[:], in0=v[:], scalar1=NEG_SLOPE - 1.0, scalar2=0.0,
                                     op0=ALU.mult, op1=ALU.add)
-            m2 = f32_pool.tile([P, P * PACK], F32, name="m2")
+            m2 = f32_pool.tile([P, G_TOKENS * PACK], F32, name="m2")
             nc.gpsimd.tensor_scalar(out=m2[:], in0=m1[:], scalar1=F32_MAX, scalar2=0.0,
                                     op0=ALU.min, op1=ALU.max)
-            nc.gpsimd.tensor_tensor(out=grouped_of(quad)[:, 0, 0].rearrange("p n t -> p (n t)"),
+            dst = grouped_of(quad)[:, 0, 0, 0:G_TOKENS, :]
+            nc.gpsimd.tensor_tensor(out=dst.rearrange("p n t -> p (n t)"),
                                     in0=v[:], in1=m2[:], op=ALU.add)
 
         def quantise(step, lo, hi):

from contextlib import ExitStack

import concourse.mybir as mybir
from concourse.masks import make_identity

F32 = mybir.dt.float32
BF16 = mybir.dt.bfloat16
U32 = mybir.dt.uint32
U8 = mybir.dt.uint8
FP8X4 = mybir.dt.float8_e4m3fn_x4
ALU = mybir.AluOpType
ACT = mybir.ActivationFunctionType

E, N, D, H = 4, 2048, 128, 512
P = 128
PACK = 4
NEG_SLOPE = 0.01
F32_MAX = 3.4028234663852886e38
FLOPS = 2 * E * N * (D * H + H * H + H * D)

GROUPS = N // P
GQ = 4
QE = GROUPS // GQ
NQ = E * QE
H_BANKS = 6
G_FIRST = 4
G_TOKENS = 96
OC_ON_VECTOR = ()


def tile_mlpexperts_t_kernel(tc, x, w1, w2, w3, out):
    nc = tc.nc
    with ExitStack() as ctx:
        const = ctx.enter_context(tc.tile_pool(name="const", bufs=1))
        xt_pool = ctx.enter_context(tc.tile_pool(name="xtp", bufs=2))
        cast_pool = ctx.enter_context(tc.tile_pool(name="yp", bufs=8))
        f32_pool = ctx.enter_context(tc.tile_pool(name="vp", bufs=2))
        grouped_pool = ctx.enter_context(tc.tile_pool(name="gp", bufs=2))
        codes_pool = ctx.enter_context(tc.tile_pool(name="qp", bufs=3))
        out_pool = ctx.enter_context(tc.tile_pool(name="op", bufs=6))
        ps_h = ctx.enter_context(tc.psum_pool(name="ps_h", bufs=H_BANKS))
        ps_x = ctx.enter_context(tc.psum_pool(name="ps_x", bufs=1))
        ps_o = ctx.enter_context(tc.psum_pool(name="ps_o", bufs=1))
        ctx.enter_context(tc.manual_schedule())

        warm_in = const.tile([P, 1], F32, name="warm_in")
        warm_out = const.tile([P, 1], F32, name="warm_out")
        nc.vector.memset(warm_in[:], 0.0)
        nc.scalar.activation(out=warm_out[:], in_=warm_in[:], func=ACT.Copy, scale=NEG_SLOPE)

        ident = const.tile([P, P], BF16, name="ident")
        make_identity(nc, ident[:])

        x_sb = [const.tile([P, GROUPS, D], BF16, name="x_sb%d" % e) for e in range(E)]
        w1_sb = const.tile([P, E, H], BF16, name="w1_sb")
        w2_raw = [const.tile([P, PACK, H], BF16, name="w2_raw%d" % e) for e in range(E)]
        w3_raw = const.tile([P, E, PACK, D], BF16, name="w3_raw")
        w2_grouped = [const.tile([P, H, PACK], BF16, name="w2g%d" % e, align_bytes=64)
                      for e in range(E)]
        w3_grouped = const.tile([P, E, D, PACK], BF16, name="w3g", align_bytes=64)
        w2_words = [const.tile([P, H], U32, name="w2q%d" % e, align_bytes=64) for e in range(E)]
        w2_scales = [const.tile([P, H], U8, name="w2s%d" % e, align_bytes=64) for e in range(E)]
        w3_words = const.tile([P, E * D], U32, name="w3q", align_bytes=64)
        w3_scales = const.tile([P, E * D], U8, name="w3s", align_bytes=64)

        x_view = [x[e].rearrange("(p j) d -> p j d", j=GROUPS) for e in range(E)]
        out_view = [out[e].rearrange("(p j) d -> p j d", j=GROUPS) for e in range(E)]
        w1_view = w1.rearrange("e d h -> d e h")

        def load_w2(e):
            nc.sync.dma_start(out=w2_raw[e][:], in_=w2[e].rearrange("(t p) m -> p t m", p=P))

        nc.sync.dma_start(out=x_sb[0][:, 0:GQ, :], in_=x_view[0][:, 0:GQ, :])
        nc.sync.dma_start(out=w1_sb[:, 0, :], in_=w1_view[:, 0, :])
        load_w2(0)
        nc.sync.dma_start(out=x_sb[0][:, GQ:GROUPS, :], in_=x_view[0][:, GQ:GROUPS, :])
        nc.sync.dma_start(out=w3_raw[:], in_=w3.rearrange("e (t p) n -> p e t n", p=P))
        nc.sync.dma_start(out=w1_sb[:, 1:E, :], in_=w1_view[:, 1:E, :])
        for e in range(1, E):
            load_w2(e)
            nc.sync.dma_start(out=x_sb[e][:], in_=x_view[e])

        def regroup(dst, src):
            nc.gpsimd.tensor_scalar(out=dst, in0=src.rearrange("p t c -> p c t"),
                                    scalar1=1.0, scalar2=0.0, op0=ALU.mult, op1=ALU.add)

        def regroup_w2(e):
            for c in range(PACK):
                cols = slice(c * P, (c + 1) * P)
                regroup(w2_grouped[e][:, cols, :], w2_raw[e][:, :, cols])

        def quantise_w2(e):
            nc.vector.quantize_mx(out=w2_words[e][:].bitcast(FP8X4), scales=w2_scales[e][:],
                                  in_=w2_grouped[e][:].rearrange("p m t -> p (m t)"))

        def quantise_w3():
            nc.vector.quantize_mx(out=w3_words[:].bitcast(FP8X4), scales=w3_scales[:],
                                  in_=w3_grouped[:].rearrange("p e n t -> p (e n t)"))

        x_t = {}
        grouped = {}
        codes = {}
        f32_copy = {}

        def grouped_of(step):
            if step not in grouped:
                grouped[step] = grouped_pool.tile([P, 2, GQ, P, PACK], BF16, name="gg",
                                                  align_bytes=64)
            return grouped[step]

        def codes_of(step):
            if step not in codes:
                words = codes_pool.tile([P, 2 * GQ * P], U32, name="hq", align_bytes=64)
                scales = codes_pool.tile([P, 2 * GQ * P], U8, name="hs", align_bytes=64)
                codes[step] = (words, scales)
            return codes[step]

        def transpose_x(quad, first, n, pool, tag):
            e, q = divmod(quad, QE)
            if first == 0:
                x_t[quad] = xt_pool.tile([P, GQ, P], BF16, name="xT")
            xt_ps = pool.tile([P, n, P], BF16, name="xt_ps", tag=tag)
            for g in range(n):
                nc.tensor.transpose(xt_ps[:, g, :], x_sb[e][:, q * GQ + first + g, :], ident[:])
            nc.scalar.copy(out=x_t[quad][:, first:first + n, :], in_=xt_ps[:])

        def lrelu(bank, dst, first=0):
            v = bank[:].rearrange("p t n -> p n t")[:, first:P, :]
            cast = cast_pool.tile([P, P - first, PACK], BF16, name="y")
            nc.scalar.copy(out=cast[:], in_=v)
            nc.vector.scalar_tensor_tensor(out=dst[:, first:P, :], in0=v, scalar=NEG_SLOPE,
                                           in1=cast[:], op0=ALU.mult, op1=ALU.max)

        def layer1(quad, g):
            e = quad // QE
            bank = ps_h.tile([P, PACK, P], F32, name="hb")
            for t in range(PACK):
                nc.tensor.matmul(bank[:, t, :], lhsT=w1_sb[:, e, t * P:(t + 1) * P],
                                 rhs=x_t[quad][:, g, :], start=True, stop=True)
            if g == 0 and quad >= G_FIRST:
                f32_copy[quad] = f32_pool.tile([P, G_TOKENS * PACK], F32, name="vs")
                nc.scalar.copy(out=f32_copy[quad][:].rearrange("p (n t) -> p n t", t=PACK),
                               in_=bank[:].rearrange("p t n -> p n t")[:, 0:G_TOKENS, :])
                lrelu(bank, grouped_of(quad)[:, 0, g], G_TOKENS)
            else:
                lrelu(bank, grouped_of(quad)[:, 0, g])

        def lrelu_on_gpsimd(quad):
            nc.gpsimd.memset(grouped[quad - 1][:, 0, 0, 0, 0:2], 0.0)
            v = f32_copy[quad]
            m1 = f32_pool.tile([P, G_TOKENS * PACK], F32, name="m1")
            nc.gpsimd.tensor_scalar(out=m1[:], in0=v[:], scalar1=NEG_SLOPE - 1.0, scalar2=0.0,
                                    op0=ALU.mult, op1=ALU.add)
            m2 = f32_pool.tile([P, G_TOKENS * PACK], F32, name="m2")
            nc.gpsimd.tensor_scalar(out=m2[:], in0=m1[:], scalar1=F32_MAX, scalar2=0.0,
                                    op0=ALU.min, op1=ALU.max)
            dst = grouped_of(quad)[:, 0, 0, 0:G_TOKENS, :]
            nc.gpsimd.tensor_tensor(out=dst.rearrange("p n t -> p (n t)"),
                                    in0=v[:], in1=m2[:], op=ALU.add)

        def quantise(step, lo, hi):
            words, scales = codes_of(step)
            cols = slice(lo * P, hi * P)
            src = grouped[step][:].rearrange("p s j n t -> p (s j) (n t)")
            nc.vector.quantize_mx(out=words[:, cols].bitcast(FP8X4), scales=scales[:, cols],
                                  in_=src[:, lo:hi, :].rearrange("p j c -> p (j c)"))

        def layer2(quad, g):
            e = quad // QE
            words, scales = codes[quad]
            tokens = slice(g * P, (g + 1) * P)
            bank = ps_h.tile([P, PACK, P], F32, name="hb")
            for t in range(PACK):
                chunk = slice(t * P, (t + 1) * P)
                nc.tensor.matmul_mx(out=bank[:, t, :],
                                    lhsT=w2_words[e][:, chunk].bitcast(FP8X4),
                                    lhsT_scale=w2_scales[e][:, chunk],
                                    rhs=words[:, tokens].bitcast(FP8X4),
                                    rhs_scale=scales[:, tokens],
                                    start=True, stop=True)
            lrelu(bank, grouped_of(quad + 2)[:, 1, g])

        def layer3(quad, first, n, pool, tag):
            e, q = divmod(quad, QE)
            words, scales = codes[quad + 2]
            w_cols = slice(e * D, (e + 1) * D)
            o_ps = pool.tile([P, n, D], F32, name="o_ps", tag=tag)
            for g in range(n):
                tokens = slice((GQ + first + g) * P, (GQ + first + g + 1) * P)
                nc.tensor.matmul_mx(out=o_ps[:, g, :],
                                    lhsT=words[:, tokens].bitcast(FP8X4),
                                    lhsT_scale=scales[:, tokens],
                                    rhs=w3_words[:, w_cols].bitcast(FP8X4),
                                    rhs_scale=w3_scales[:, w_cols],
                                    start=True, stop=True)
            o_sb = out_pool.tile([P, n, D], F32, name="o_sb")
            if quad in OC_ON_VECTOR:
                nc.vector.tensor_copy(out=o_sb[:], in_=o_ps[:])
            else:
                nc.scalar.copy(out=o_sb[:], in_=o_ps[:])
            j0 = q * GQ + first
            nc.sync.dma_start(out=out_view[e][:, j0:j0 + n, :], in_=o_sb[:])

        regroup_w2(0)
        for e in range(E):
            regroup(w3_grouped[:, e], w3_raw[:, e])
        for e in range(1, E):
            regroup_w2(e)

        transpose_x(0, 0, 1, ps_h, "hb")
        transpose_x(0, 1, GQ - 1, ps_h, "hb")

        LAST = NQ + 1
        for i in range(LAST + 1):
            units = []
            if i < NQ:
                units.extend([(1, i, g) for g in range(GQ)])
            if 0 <= i - 2:
                units.extend([(2, i - 2, g) for g in range(GQ)])
            for k, (layer, quad, g) in enumerate(units):
                if layer == 1:
                    layer1(quad, g)
                else:
                    layer2(quad, g)
                if k == 1:
                    if i == 1:
                        quantise_w2(0)
                    if i == 3:
                        quantise_w3()
                    if i % QE == 0 and 0 < i < NQ:
                        quantise_w2(i // QE)
                    if i >= 1:
                        lo = 0 if i - 1 < NQ else GQ
                        hi = 2 * GQ if i - 3 >= 0 else GQ
                        quantise(i - 1, lo, hi)
                    if G_FIRST <= i < NQ:
                        lrelu_on_gpsimd(i)
                if layer == 1 and g == GQ - 1 and i + 1 < NQ:
                    transpose_x(i + 1, 0, GQ, ps_x, "xt_ps")
                if i == LAST and k >= 1:
                    quantise(LAST, GQ + k - 1, GQ + k)
            if 0 <= i - 3:
                layer3(i - 3, 0, GQ, ps_o, "o_ps")
        quantise(LAST, 2 * GQ - 1, 2 * GQ)
        for g in range(GQ):
            layer3(NQ - 1, g, 1, ps_h, "hb")
